import numpy as np
import ml_dtypes


def mxq(x, axis, fmt="e4m3"):
    dtype, down = {"e4m3": (ml_dtypes.float8_e4m3fn, 7), "e5m2": (ml_dtypes.float8_e5m2, 14)}[fmt]
    v = np.moveaxis(np.asarray(x, np.float32).astype(ml_dtypes.bfloat16).astype(np.float64), axis, -1)
    blocks = v.reshape(v.shape[:-1] + (-1, 32))
    amax = np.abs(blocks).max(-1, keepdims=True)
    byte = np.maximum(np.where(amax > 0, np.frexp(amax)[1] - 1 + 127, 0) - down, 1)
    scale = np.exp2(byte - 127.0)
    codes = (blocks / scale).astype(np.float32).astype(dtype).astype(np.float64)
    return np.moveaxis((codes * scale).reshape(v.shape), -1, axis)


WIDE = False


def mx_kscale(k):
    if not WIDE:
        return np.ones(k)
    levels = np.array([10, -10, 5, -5, 0])
    a = np.random.permutation(np.resize(levels, k // 512 * 4)).reshape(k // 512, 4)
    idx = np.arange(k)
    return np.exp2(a[idx // 512, idx % 128 // 32])


BF16 = ml_dtypes.bfloat16


def bf(x):
    return np.asarray(x, np.float32).astype(BF16)


def f64(x):
    return np.asarray(x).astype(np.float64)


B, IN_F, OUT_F = 128, 65536, 512
IN_Q = IN_F // 4
OUT_Q = OUT_F // 4


def setup_inputs():
    s = mx_kscale(IN_Q)
    scale = 1.0 / np.sqrt(IN_Q)
    inp = {"x": bf((np.random.standard_normal((B, 4, IN_Q)) * s).reshape(B, IN_F))}
    for name in ["rr", "ri", "rj", "rk"]:
        inp["W_" + name] = bf(np.random.uniform(-scale, scale, (OUT_Q, IN_Q)) / s[None, :])
    for name in ["rr", "ri", "rj", "rk"]:
        inp["b_" + name] = bf(np.random.standard_normal(OUT_Q) * 0.5)
    return inp


def reference(x, W_rr, W_ri, W_rj, W_rk, b_rr, b_ri, b_rj, b_rk):
    b = x.shape[0]
    xs = f64(x).reshape(b, 4, IN_Q)
    W = np.stack([f64(W_rr), f64(W_ri), f64(W_rj), f64(W_rk)])
    bias = np.stack([f64(b_rr), f64(b_ri), f64(b_rj), f64(b_rk)])
    xq = mxq(xs, 2, "e4m3")
    Wq = mxq(W, 2, "e4m3")
    Y = (xq.reshape(b * 4, IN_Q) @ Wq.reshape(4 * OUT_Q, IN_Q).T).reshape(b, 4, 4, OUT_Q) + bias
    out_r = Y[:, 0, 0] - Y[:, 1, 1] - Y[:, 2, 2] - Y[:, 3, 3]
    out_i = Y[:, 0, 1] + Y[:, 1, 0] + Y[:, 2, 3] - Y[:, 3, 2]
    out_j = Y[:, 0, 2] - Y[:, 1, 3] + Y[:, 2, 0] + Y[:, 3, 1]
    out_k = Y[:, 0, 3] + Y[:, 1, 2] - Y[:, 2, 1] + Y[:, 3, 0]
    out = np.stack([out_r, out_i, out_j, out_k], axis=1)
    return out.reshape(b, -1)

@@ -1,0 +1,167 @@
+from contextlib import ExitStack
+
+import concourse.masks as masks
+import concourse.mybir as mybir
+
+F32 = mybir.dt.float32
+BF16 = mybir.dt.bfloat16
+U32 = mybir.dt.uint32
+U8 = mybir.dt.uint8
+FP8X4 = mybir.dt.float8_e4m3fn_x4
+ADD = mybir.AluOpType.add
+SUBTRACT = mybir.AluOpType.subtract
+
+P = 128
+MEMBERS = 4
+K = 16384
+PACK = 4
+K_PASS = P * PACK
+PASSES = K // K_PASS
+HALVES = 2
+K_HALF = K_PASS // HALVES
+BANK_WORDS = 512
+BANK_MEMBERS = BANK_WORDS // (HALVES * P)
+
+STAGE_PASSES = 2
+STAGES = PASSES // STAGE_PASSES
+STAGE_COLS = STAGE_PASSES * K_PASS
+RAW_BUFS = 6
+VECTOR_EVERY = 4
+
+SIGN = (
+    (1, -1, -1, -1),
+    (1, 1, 1, -1),
+    (1, -1, 1, 1),
+    (1, 1, -1, 1),
+)
+
+FLOPS = 2 * (MEMBERS * P) * (MEMBERS * P) * K
+
+
+def tile_qdense_k_kernel(
+    tc, x, W_rr, W_ri, W_rj, W_rk, b_rr, b_ri, b_rj, b_rk, out
+):
+    nc = tc.nc
+    x_chunks = x.rearrange("b (c k) -> b c k", c=MEMBERS)
+    weights = (W_rr, W_ri, W_rj, W_rk)
+    biases = (b_rr, b_ri, b_rj, b_rk)
+
+    with ExitStack() as ctx:
+        ctx.enter_context(tc.manual_schedule())
+        const = ctx.enter_context(tc.tile_pool(name="const", bufs=1))
+        raw_pool = ctx.enter_context(tc.tile_pool(name="raw", bufs=RAW_BUFS))
+        grouped_pool = ctx.enter_context(tc.tile_pool(name="grouped", bufs=4))
+        code_pool = ctx.enter_context(tc.tile_pool(name="codes", bufs=3))
+        product_pool = ctx.enter_context(tc.psum_pool(name="products", bufs=1))
+        bank_pool = ctx.enter_context(tc.psum_pool(name="banks", bufs=4))
+
+        def add_chunk(total, terms, c):
+            for j in range(MEMBERS):
+                nc.vector.tensor_tensor(
+                    out=total[:, j, :],
+                    in0=total[:, j, :],
+                    in1=terms[:, j ^ c, :],
+                    op=ADD if SIGN[j][c] > 0 else SUBTRACT,
+                )
+
+        identity = const.tile([P, P], F32)
+        masks.make_identity(nc, identity[:])
+
+        ones = const.tile([P, P], BF16)
+        nc.vector.memset(ones[:], 1.0)
+        bias_rows = const.tile([P, MEMBERS, P], BF16)
+        nc.vector.memset(bias_rows[:], 0.0)
+        for q in range(MEMBERS):
+            nc.scalar.dma_start(out=bias_rows[0:1, q, :], in_=biases[q].unsqueeze(0))
+        bias_bank = bank_pool.tile([P, MEMBERS, P], F32, tag="bank")
+        nc.tensor.matmul(
+            out=bias_bank[:].rearrange("p q o -> p (q o)"),
+            lhsT=ones[:],
+            rhs=bias_rows[:].rearrange("p q o -> p (q o)"),
+            start=True,
+            stop=True,
+        )
+        total = const.tile([P, MEMBERS, P], F32)
+        nc.vector.tensor_copy(out=total[:], in_=bias_bank[:])
+        for c in range(1, MEMBERS):
+            add_chunk(total, bias_bank, c)
+
+        products = [
+            product_pool.tile([P, MEMBERS, P], F32, name="products%d" % c)
+            for c in range(MEMBERS)
+        ]
+
+        def transpose_pass(raw, pass_in_stage, unit):
+            grouped = grouped_pool.tile([P, MEMBERS * P * PACK], BF16, align_bytes=64)
+            grouped_words = grouped[:].bitcast(F32)
+            for b in range(MEMBERS // BANK_MEMBERS):
+                bank = bank_pool.tile([P, BANK_MEMBERS, HALVES, P], F32, tag="bank")
+                for i in range(BANK_MEMBERS):
+                    for u in range(HALVES):
+                        first = pass_in_stage * K_PASS + u * K_HALF
+                        nc.tensor.transpose(
+                            bank[:, i, u, :],
+                            raw[:, b * BANK_MEMBERS + i, first : first + K_HALF].bitcast(F32),
+                            identity[:],
+                        )
+                bank_number = unit * (MEMBERS // BANK_MEMBERS) + b
+                to_vector = bank_number % VECTOR_EVERY == VECTOR_EVERY - 1
+                copy_out = nc.vector.tensor_copy if to_vector else nc.scalar.copy
+                copy_out(
+                    out=grouped_words[:, b * BANK_WORDS : (b + 1) * BANK_WORDS].rearrange(
+                        "p (i r u) -> p i r u", i=BANK_MEMBERS, u=HALVES
+                    ),
+                    in_=bank[:].rearrange("p i u r -> p i r u"),
+                )
+            return grouped
+
+        def quantise(grouped, codes, scales):
+            nc.vector.quantize_mx(out=codes.bitcast(FP8X4), scales=scales, in_=grouped[:])
+
+        def multiply(stage, x_codes, x_scales, w_codes, w_scales):
+            for c in range(MEMBERS):
+                rows = slice(c * P, (c + 1) * P)
+                for g in range(STAGE_PASSES):
+                    number = stage * STAGE_PASSES + g
+                    nc.tensor.matmul_mx(
+                        out=products[c][:].rearrange("p q o -> p (q o)"),
+                        lhsT=x_codes[:, g, rows].bitcast(FP8X4),
+                        lhsT_scale=x_scales[:, g, rows],
+                        rhs=w_codes[:, g, :].bitcast(FP8X4),
+                        rhs_scale=w_scales[:, g, :],
+                        start=(number == 0),
+                        stop=(number == PASSES - 1),
+                    )
+
+        waiting = None
+        ready = None
+        unit = 0
+        for stage in range(STAGES):
+            cols = slice(stage * STAGE_COLS, (stage + 1) * STAGE_COLS)
+            x_raw = raw_pool.tile([P, MEMBERS, STAGE_COLS], BF16)
+            nc.sync.dma_start(out=x_raw[:], in_=x_chunks[:, :, cols])
+            w_raw = raw_pool.tile([P, MEMBERS, STAGE_COLS], BF16)
+            for q in range(MEMBERS):
+                nc.sync.dma_start(out=w_raw[:, q, :], in_=weights[q][:, cols])
+
+            x_codes = code_pool.tile([P, STAGE_PASSES, MEMBERS * P], U32, align_bytes=64)
+            x_scales = code_pool.tile([P, STAGE_PASSES, MEMBERS * P], U8, align_bytes=64)
+            w_codes = code_pool.tile([P, STAGE_PASSES, MEMBERS * P], U32, align_bytes=64)
+            w_scales = code_pool.tile([P, STAGE_PASSES, MEMBERS * P], U8, align_bytes=64)
+
+            for raw, codes, scales in ((x_raw, x_codes, x_scales), (w_raw, w_codes, w_scales)):
+                for g in range(STAGE_PASSES):
+                    grouped = transpose_pass(raw, g, unit)
+                    unit += 1
+                    if waiting is not None:
+                        quantise(*waiting)
+                    waiting = (grouped, codes[:, g, :], scales[:, g, :])
+            if ready is not None:
+                multiply(stage - 1, *ready)
+            ready = (x_codes, x_scales, w_codes, w_scales)
+        quantise(*waiting)
+        multiply(STAGES - 1, *ready)
+
+        for c in range(MEMBERS):
+            add_chunk(total, products[c], c)
+        nc.sync.dma_start(out=out, in_=total[:].rearrange("p j o -> p (j o)"))

@@ -22,9 +22,10 @@ K_HALF = K_PASS // HALVES
 BANK_WORDS = 512
 BANK_MEMBERS = BANK_WORDS // (HALVES * P)
 
-STAGE_PASSES = 2
+STAGE_PASSES = 1
 STAGES = PASSES // STAGE_PASSES
-STAGE_COLS = STAGE_PASSES * K_PASS
+LOAD_PASSES = 2
+LOAD_COLS = LOAD_PASSES * K_PASS
 RAW_BUFS = 6
 VECTOR_EVERY = 4
 
@@ -91,14 +92,14 @@ def tile_qdense_k_kernel(
             for c in range(MEMBERS)
         ]
 
-        def transpose_pass(raw, pass_in_stage, unit):
+        def transpose_pass(raw, pass_in_load, unit):
             grouped = grouped_pool.tile([P, MEMBERS * P * PACK], BF16, align_bytes=64)
             grouped_words = grouped[:].bitcast(F32)
             for b in range(MEMBERS // BANK_MEMBERS):
                 bank = bank_pool.tile([P, BANK_MEMBERS, HALVES, P], F32, tag="bank")
                 for i in range(BANK_MEMBERS):
                     for u in range(HALVES):
-                        first = pass_in_stage * K_PASS + u * K_HALF
+                        first = pass_in_load * K_PASS + u * K_HALF
                         nc.tensor.transpose(
                             bank[:, i, u, :],
                             raw[:, b * BANK_MEMBERS + i, first : first + K_HALF].bitcast(F32),
@@ -136,13 +137,17 @@ def tile_qdense_k_kernel(
         waiting = None
         ready = None
         unit = 0
+        x_raw = None
+        w_raw = None
         for stage in range(STAGES):
-            cols = slice(stage * STAGE_COLS, (stage + 1) * STAGE_COLS)
-            x_raw = raw_pool.tile([P, MEMBERS, STAGE_COLS], BF16)
-            nc.sync.dma_start(out=x_raw[:], in_=x_chunks[:, :, cols])
-            w_raw = raw_pool.tile([P, MEMBERS, STAGE_COLS], BF16)
-            for q in range(MEMBERS):
-                nc.sync.dma_start(out=w_raw[:, q, :], in_=weights[q][:, cols])
+            first_pass = stage * STAGE_PASSES
+            if first_pass % LOAD_PASSES == 0:
+                cols = slice(first_pass * K_PASS, first_pass * K_PASS + LOAD_COLS)
+                x_raw = raw_pool.tile([P, MEMBERS, LOAD_COLS], BF16, name="x_raw")
+                nc.sync.dma_start(out=x_raw[:], in_=x_chunks[:, :, cols])
+                w_raw = raw_pool.tile([P, MEMBERS, LOAD_COLS], BF16, name="w_raw")
+                for q in range(MEMBERS):
+                    nc.sync.dma_start(out=w_raw[:, q, :], in_=weights[q][:, cols])
 
             x_codes = code_pool.tile([P, STAGE_PASSES, MEMBERS * P], U32, align_bytes=64)
             x_scales = code_pool.tile([P, STAGE_PASSES, MEMBERS * P], U8, align_bytes=64)
@@ -151,7 +156,7 @@ def tile_qdense_k_kernel(
 
             for raw, codes, scales in ((x_raw, x_codes, x_scales), (w_raw, w_codes, w_scales)):
                 for g in range(STAGE_PASSES):
-                    grouped = transpose_pass(raw, g, unit)
+                    grouped = transpose_pass(raw, (first_pass + g) % LOAD_PASSES, unit)
                     unit += 1
                     if waiting is not None:
                         quantise(*waiting)

@@ -24,9 +24,9 @@ BANK_MEMBERS = BANK_WORDS // (HALVES * P)
 
 STAGE_PASSES = 1
 STAGES = PASSES // STAGE_PASSES
-LOAD_PASSES = 2
+LOAD_PASSES = 4
 LOAD_COLS = LOAD_PASSES * K_PASS
-RAW_BUFS = 6
+RAW_BUFS = 4
 VECTOR_EVERY = 4
 
 SIGN = (

@@ -24,10 +24,11 @@ BANK_MEMBERS = BANK_WORDS // (HALVES * P)
 
 STAGE_PASSES = 1
 STAGES = PASSES // STAGE_PASSES
-LOAD_PASSES = 4
+LOAD_PASSES = 2
 LOAD_COLS = LOAD_PASSES * K_PASS
-RAW_BUFS = 4
+RAW_BUFS = 6
 VECTOR_EVERY = 4
+MX_LAG = 2
 
 SIGN = (
     (1, -1, -1, -1),
@@ -52,7 +53,7 @@ def tile_qdense_k_kernel(
         const = ctx.enter_context(tc.tile_pool(name="const", bufs=1))
         raw_pool = ctx.enter_context(tc.tile_pool(name="raw", bufs=RAW_BUFS))
         grouped_pool = ctx.enter_context(tc.tile_pool(name="grouped", bufs=4))
-        code_pool = ctx.enter_context(tc.tile_pool(name="codes", bufs=3))
+        code_pool = ctx.enter_context(tc.tile_pool(name="codes", bufs=MX_LAG + 2))
         product_pool = ctx.enter_context(tc.psum_pool(name="products", bufs=1))
         bank_pool = ctx.enter_context(tc.psum_pool(name="banks", bufs=4))
 
@@ -135,7 +136,7 @@ def tile_qdense_k_kernel(
                     )
 
         waiting = None
-        ready = None
+        operands = []
         unit = 0
         x_raw = None
         w_raw = None
@@ -161,11 +162,12 @@ def tile_qdense_k_kernel(
                     if waiting is not None:
                         quantise(*waiting)
                     waiting = (grouped, codes[:, g, :], scales[:, g, :])
-            if ready is not None:
-                multiply(stage - 1, *ready)
-            ready = (x_codes, x_scales, w_codes, w_scales)
+            operands.append((stage, x_codes, x_scales, w_codes, w_scales))
+            if stage >= MX_LAG:
+                multiply(*operands[stage - MX_LAG])
         quantise(*waiting)
-        multiply(STAGES - 1, *ready)
+        for stage in range(STAGES - MX_LAG, STAGES):
+            multiply(*operands[stage])
 
         for c in range(MEMBERS):
             add_chunk(total, products[c], c)

from contextlib import ExitStack

import concourse.masks as masks
import concourse.mybir as mybir

F32 = mybir.dt.float32
BF16 = mybir.dt.bfloat16
U32 = mybir.dt.uint32
U8 = mybir.dt.uint8
FP8X4 = mybir.dt.float8_e4m3fn_x4
ADD = mybir.AluOpType.add
SUBTRACT = mybir.AluOpType.subtract

P = 128
MEMBERS = 4
K = 16384
PACK = 4
K_PASS = P * PACK
PASSES = K // K_PASS
HALVES = 2
K_HALF = K_PASS // HALVES
BANK_WORDS = 512
BANK_MEMBERS = BANK_WORDS // (HALVES * P)

STAGE_PASSES = 1
STAGES = PASSES // STAGE_PASSES
LOAD_PASSES = 2
LOAD_COLS = LOAD_PASSES * K_PASS
RAW_BUFS = 6
VECTOR_EVERY = 4
MX_LAG = 2

SIGN = (
    (1, -1, -1, -1),
    (1, 1, 1, -1),
    (1, -1, 1, 1),
    (1, 1, -1, 1),
)

FLOPS = 2 * (MEMBERS * P) * (MEMBERS * P) * K


def tile_qdense_k_kernel(
    tc, x, W_rr, W_ri, W_rj, W_rk, b_rr, b_ri, b_rj, b_rk, out
):
    nc = tc.nc
    x_chunks = x.rearrange("b (c k) -> b c k", c=MEMBERS)
    weights = (W_rr, W_ri, W_rj, W_rk)
    biases = (b_rr, b_ri, b_rj, b_rk)

    with ExitStack() as ctx:
        ctx.enter_context(tc.manual_schedule())
        const = ctx.enter_context(tc.tile_pool(name="const", bufs=1))
        raw_pool = ctx.enter_context(tc.tile_pool(name="raw", bufs=RAW_BUFS))
        grouped_pool = ctx.enter_context(tc.tile_pool(name="grouped", bufs=4))
        code_pool = ctx.enter_context(tc.tile_pool(name="codes", bufs=MX_LAG + 2))
        product_pool = ctx.enter_context(tc.psum_pool(name="products", bufs=1))
        bank_pool = ctx.enter_context(tc.psum_pool(name="banks", bufs=4))

        def add_chunk(total, terms, c):
            for j in range(MEMBERS):
                nc.vector.tensor_tensor(
                    out=total[:, j, :],
                    in0=total[:, j, :],
                    in1=terms[:, j ^ c, :],
                    op=ADD if SIGN[j][c] > 0 else SUBTRACT,
                )

        identity = const.tile([P, P], F32)
        masks.make_identity(nc, identity[:])

        ones = const.tile([P, P], BF16)
        nc.vector.memset(ones[:], 1.0)
        bias_rows = const.tile([P, MEMBERS, P], BF16)
        nc.vector.memset(bias_rows[:], 0.0)
        for q in range(MEMBERS):
            nc.scalar.dma_start(out=bias_rows[0:1, q, :], in_=biases[q].unsqueeze(0))
        bias_bank = bank_pool.tile([P, MEMBERS, P], F32, tag="bank")
        nc.tensor.matmul(
            out=bias_bank[:].rearrange("p q o -> p (q o)"),
            lhsT=ones[:],
            rhs=bias_rows[:].rearrange("p q o -> p (q o)"),
            start=True,
            stop=True,
        )
        total = const.tile([P, MEMBERS, P], F32)
        nc.vector.tensor_copy(out=total[:], in_=bias_bank[:])
        for c in range(1, MEMBERS):
            add_chunk(total, bias_bank, c)

        products = [
            product_pool.tile([P, MEMBERS, P], F32, name="products%d" % c)
            for c in range(MEMBERS)
        ]

        def transpose_pass(raw, pass_in_load, unit):
            grouped = grouped_pool.tile([P, MEMBERS * P * PACK], BF16, align_bytes=64)
            grouped_words = grouped[:].bitcast(F32)
            for b in range(MEMBERS // BANK_MEMBERS):
                bank = bank_pool.tile([P, BANK_MEMBERS, HALVES, P], F32, tag="bank")
                for i in range(BANK_MEMBERS):
                    for u in range(HALVES):
                        first = pass_in_load * K_PASS + u * K_HALF
                        nc.tensor.transpose(
                            bank[:, i, u, :],
                            raw[:, b * BANK_MEMBERS + i, first : first + K_HALF].bitcast(F32),
                            identity[:],
                        )
                bank_number = unit * (MEMBERS // BANK_MEMBERS) + b
                to_vector = bank_number % VECTOR_EVERY == VECTOR_EVERY - 1
                copy_out = nc.vector.tensor_copy if to_vector else nc.scalar.copy
                copy_out(
                    out=grouped_words[:, b * BANK_WORDS : (b + 1) * BANK_WORDS].rearrange(
                        "p (i r u) -> p i r u", i=BANK_MEMBERS, u=HALVES
                    ),
                    in_=bank[:].rearrange("p i u r -> p i r u"),
                )
            return grouped

        def quantise(grouped, codes, scales):
            nc.vector.quantize_mx(out=codes.bitcast(FP8X4), scales=scales, in_=grouped[:])

        def multiply(stage, x_codes, x_scales, w_codes, w_scales):
            for c in range(MEMBERS):
                rows = slice(c * P, (c + 1) * P)
                for g in range(STAGE_PASSES):
                    number = stage * STAGE_PASSES + g
                    nc.tensor.matmul_mx(
                        out=products[c][:].rearrange("p q o -> p (q o)"),
                        lhsT=x_codes[:, g, rows].bitcast(FP8X4),
                        lhsT_scale=x_scales[:, g, rows],
                        rhs=w_codes[:, g, :].bitcast(FP8X4),
                        rhs_scale=w_scales[:, g, :],
                        start=(number == 0),
                        stop=(number == PASSES - 1),
                    )

        waiting = None
        operands = []
        unit = 0
        x_raw = None
        w_raw = None
        for stage in range(STAGES):
            first_pass = stage * STAGE_PASSES
            if first_pass % LOAD_PASSES == 0:
                cols = slice(first_pass * K_PASS, first_pass * K_PASS + LOAD_COLS)
                x_raw = raw_pool.tile([P, MEMBERS, LOAD_COLS], BF16, name="x_raw")
                nc.sync.dma_start(out=x_raw[:], in_=x_chunks[:, :, cols])
                w_raw = raw_pool.tile([P, MEMBERS, LOAD_COLS], BF16, name="w_raw")
                for q in range(MEMBERS):
                    nc.sync.dma_start(out=w_raw[:, q, :], in_=weights[q][:, cols])

            x_codes = code_pool.tile([P, STAGE_PASSES, MEMBERS * P], U32, align_bytes=64)
            x_scales = code_pool.tile([P, STAGE_PASSES, MEMBERS * P], U8, align_bytes=64)
            w_codes = code_pool.tile([P, STAGE_PASSES, MEMBERS * P], U32, align_bytes=64)
            w_scales = code_pool.tile([P, STAGE_PASSES, MEMBERS * P], U8, align_bytes=64)

            for raw, codes, scales in ((x_raw, x_codes, x_scales), (w_raw, w_codes, w_scales)):
                for g in range(STAGE_PASSES):
                    grouped = transpose_pass(raw, (first_pass + g) % LOAD_PASSES, unit)
                    unit += 1
                    if waiting is not None:
                        quantise(*waiting)
                    waiting = (grouped, codes[:, g, :], scales[:, g, :])
            operands.append((stage, x_codes, x_scales, w_codes, w_scales))
            if stage >= MX_LAG:
                multiply(*operands[stage - MX_LAG])
        quantise(*waiting)
        for stage in range(STAGES - MX_LAG, STAGES):
            multiply(*operands[stage])

        for c in range(MEMBERS):
            add_chunk(total, products[c], c)
        nc.sync.dma_start(out=out, in_=total[:].rearrange("p j o -> p (j o)"))
